import numpy as np
import ml_dtypes


def mxq(x, axis, fmt="e4m3"):
    dtype, down = {"e4m3": (ml_dtypes.float8_e4m3fn, 7), "e5m2": (ml_dtypes.float8_e5m2, 14)}[fmt]
    v = np.moveaxis(np.asarray(x, np.float32).astype(ml_dtypes.bfloat16).astype(np.float64), axis, -1)
    blocks = v.reshape(v.shape[:-1] + (-1, 32))
    amax = np.abs(blocks).max(-1, keepdims=True)
    byte = np.maximum(np.where(amax > 0, np.frexp(amax)[1] - 1 + 127, 0) - down, 1)
    scale = np.exp2(byte - 127.0)
    codes = (blocks / scale).astype(np.float32).astype(dtype).astype(np.float64)
    return np.moveaxis((codes * scale).reshape(v.shape), -1, axis)


WIDE = False


def mx_kscale(k):
    if not WIDE:
        return np.ones(k)
    levels = np.array([20, -20, 10, -10, 0])
    a = np.random.permutation(np.resize(levels, k // 512 * 4)).reshape(k // 512, 4)
    idx = np.arange(k)
    return np.exp2(a[idx // 512, idx % 128 // 32])


BF16 = ml_dtypes.bfloat16


def bf(x):
    return np.asarray(x, np.float32).astype(BF16)


def f64(x):
    return np.asarray(x).astype(np.float64)


B, D, R, P = 2048, 1024, 512, 3
GS = 4.0


def draw_u():
    return bf(np.random.standard_normal((D, R)) / np.sqrt(D))


def setup_inputs():
    s = mx_kscale(B)
    x0 = bf(np.random.standard_normal((B, D)))
    u00 = draw_u()
    u10 = draw_u()
    u11 = draw_u()
    u20 = draw_u()
    u21 = draw_u()
    u22 = draw_u()
    c = bf((1.0 + 0.25 * np.random.standard_normal(P)) / np.sqrt(R))
    beta = bf(1.0 + 0.25 * np.random.standard_normal(1))
    g = bf(np.random.standard_normal(B) * np.exp2(np.random.randint(-12, 1, B)) * GS / s)
    d21 = f64(x0) @ f64(u21)
    d22 = f64(x0) @ f64(u22)
    return {"X": bf(f64(x0) * s[:, None]),
            "U_0_0": u00, "U_1_0": u10, "U_1_1": u11,
            "U_2_0": u20, "U_2_1": u21, "U_2_2": u22,
            "C": c, "beta": beta,
            "dot_2_1": np.asarray(d21, np.float32),
            "dot_2_2": np.asarray(d22, np.float32),
            "grad_out": g}


def reference(X, U_0_0, U_1_0, U_1_1, U_2_0, U_2_1, U_2_2, C, beta, dot_2_1, dot_2_2, grad_out):
    dz = f64(grad_out)[:, None] * f64(C)[2] * f64(dot_2_1) * f64(dot_2_2)
    return mxq(f64(X), 0, "e4m3").T @ mxq(dz, 0, "e5m2")

@@ -1,0 +1,142 @@
+import concourse.mybir as mybir
+
+BF16 = mybir.dt.bfloat16
+F32 = mybir.dt.float32
+U32 = mybir.dt.uint32
+U8 = mybir.dt.uint8
+E4M3_X4 = mybir.dt.float8_e4m3fn_x4
+E5M2_X4 = mybir.dt.float8_e5m2_x4
+
+B, D, R = 2048, 1024, 512
+P = 128
+PACK = 4
+K_PASS = P * PACK
+PASSES = B // K_PASS
+M_TILE = 128
+RUN = 4
+
+LAST_PASS_PIECES = 4
+
+FLOPS = 2 * B * D * R
+BYTES = 2 * B * D + 2 * 4 * B * R + 2 * B + 2 + 4 * D * R
+
+
+def column_pieces(c):
+    pieces = LAST_PASS_PIECES if c == PASSES - 1 else 1
+    width = D // pieces
+    return [(first, width) for first in range(0, D, width)]
+
+
+def rows_by_runs(rows):
+    return rows.rearrange("p t (g i) -> p g t i", i=RUN)
+
+
+def grouped_by_runs(grouped):
+    return grouped.rearrange("p (g i) t -> p g t i", i=RUN)
+
+
+def tile_polynomialtensorregression_pa_v_kernel(
+    tc, X, U_0_0, U_1_0, U_1_1, U_2_0, U_2_1, U_2_2, C, beta, dot_2_1, dot_2_2, grad_out, out
+):
+    nc = tc.nc
+    with tc.tile_pool(name="keep", bufs=1) as keep, tc.psum_pool(name="banks", bufs=1) as banks:
+        g_rows = keep.tile([P, PASSES, PACK], BF16)
+        nc.scalar.dma_start(
+            out=g_rows[:], in_=grad_out.rearrange("(c p t) -> p c t", p=P, t=PACK)
+        )
+        c_bf16 = keep.tile([P, 3], BF16)
+        nc.scalar.dma_start(out=c_bf16[:], in_=C.partition_broadcast(P))
+
+        d1, d2, x_raw = [], [], []
+        for c in range(PASSES):
+            k_rows = slice(c * K_PASS, (c + 1) * K_PASS)
+            d1.append(keep.tile([P, PACK, R], F32, name="d1_%d" % c))
+            nc.sync.dma_start(
+                out=d1[c][:], in_=dot_2_1[k_rows, :].rearrange("(p t) r -> p t r", t=PACK)
+            )
+            d2.append(keep.tile([P, PACK, R], F32, name="d2_%d" % c))
+            nc.sync.dma_start(
+                out=d2[c][:], in_=dot_2_2[k_rows, :].rearrange("(p t) r -> p t r", t=PACK)
+            )
+            x_raw.append([])
+            for first, width in column_pieces(c):
+                piece = keep.tile([P, PACK, width], BF16, name="x_raw_%d_%d" % (c, first))
+                nc.sync.dma_start(
+                    out=piece[:],
+                    in_=X[k_rows, first : first + width].rearrange("(p t) w -> p t w", t=PACK),
+                )
+                x_raw[c].append(piece)
+
+        c_f32 = keep.tile([P, 3], F32)
+        nc.vector.tensor_copy(out=c_f32[:], in_=c_bf16[:])
+        row_factor = keep.tile([P, PASSES, PACK], F32)
+        nc.vector.tensor_scalar_mul(out=row_factor[:], in0=g_rows[:], scalar1=c_f32[:, 2:3])
+
+        acc = [banks.tile([P, R], F32, name="acc_%d" % m) for m in range(D // M_TILE)]
+
+        for c in range(PASSES):
+            for t in range(PACK):
+                nc.scalar.activation(
+                    out=d1[c][:, t, :],
+                    in_=d1[c][:, t, :],
+                    func=mybir.ActivationFunctionType.Copy,
+                    scale=row_factor[:, c, t : t + 1],
+                )
+            dz_grouped = keep.tile([P, R, PACK], BF16, name="dz_grouped_%d" % c, align_bytes=64)
+            nc.vector.tensor_tensor(
+                out=grouped_by_runs(dz_grouped[:]),
+                in0=rows_by_runs(d1[c][:]),
+                in1=rows_by_runs(d2[c][:]),
+                op=mybir.AluOpType.mult,
+            )
+            dz_codes = keep.tile([P, R], U32, name="dz_codes_%d" % c, align_bytes=64)
+            dz_scales = keep.tile([P, R], U8, name="dz_scales_%d" % c, align_bytes=64)
+            nc.vector.quantize_mx(
+                out=dz_codes[:].bitcast(E5M2_X4),
+                scales=dz_scales[:],
+                in_=dz_grouped[:].rearrange("p r t -> p (r t)"),
+            )
+
+            for piece, (first, width) in zip(x_raw[c], column_pieces(c)):
+                half = width // 2
+                x_grouped = keep.tile(
+                    [P, width, PACK], BF16, name="x_grouped_%d_%d" % (c, first), align_bytes=64
+                )
+                nc.vector.tensor_copy(
+                    out=grouped_by_runs(x_grouped[:, :half, :]),
+                    in_=rows_by_runs(piece[:, :, :half]),
+                )
+                nc.scalar.copy(
+                    out=grouped_by_runs(x_grouped[:, half:, :]),
+                    in_=rows_by_runs(piece[:, :, half:]),
+                )
+                x_codes = keep.tile(
+                    [P, width], U32, name="x_codes_%d_%d" % (c, first), align_bytes=64
+                )
+                x_scales = keep.tile(
+                    [P, width], U8, name="x_scales_%d_%d" % (c, first), align_bytes=64
+                )
+                nc.vector.quantize_mx(
+                    out=x_codes[:].bitcast(E4M3_X4),
+                    scales=x_scales[:],
+                    in_=x_grouped[:].rearrange("p w t -> p (w t)"),
+                )
+
+                for local in range(0, width, M_TILE):
+                    m = (first + local) // M_TILE
+                    nc.tensor.matmul_mx(
+                        out=acc[m][:],
+                        lhsT=x_codes[:, local : local + M_TILE].bitcast(E4M3_X4),
+                        lhsT_scale=x_scales[:, local : local + M_TILE],
+                        rhs=dz_codes[:].bitcast(E5M2_X4),
+                        rhs_scale=dz_scales[:],
+                        start=(c == 0),
+                        stop=(c == PASSES - 1),
+                    )
+                    if c == PASSES - 1:
+                        result = keep.tile([P, R], F32, name="result_%d" % m)
+                        if m % 2 == 0:
+                            nc.scalar.copy(out=result[:], in_=acc[m][:])
+                        else:
+                            nc.vector.tensor_copy(out=result[:], in_=acc[m][:])
+                        nc.sync.dma_start(out=out[m * M_TILE : (m + 1) * M_TILE, :], in_=result[:])

@@ -12,19 +12,17 @@ P = 128
 PACK = 4
 K_PASS = P * PACK
 PASSES = B // K_PASS
+LAST = PASSES - 1
 M_TILE = 128
+BANKS = D // M_TILE
 RUN = 4
-
-LAST_PASS_PIECES = 4
+PIECE = 256
+HALF = D // 2
 
 FLOPS = 2 * B * D * R
 BYTES = 2 * B * D + 2 * 4 * B * R + 2 * B + 2 + 4 * D * R
 
-
-def column_pieces(c):
-    pieces = LAST_PASS_PIECES if c == PASSES - 1 else 1
-    width = D // pieces
-    return [(first, width) for first in range(0, D, width)]
+VECTOR_EMPTIES = (5, 7)
 
 
 def rows_by_runs(rows):
@@ -39,7 +37,9 @@ def tile_polynomialtensorregression_pa_v_kernel(
     tc, X, U_0_0, U_1_0, U_1_1, U_2_0, U_2_1, U_2_2, C, beta, dot_2_1, dot_2_2, grad_out, out
 ):
     nc = tc.nc
-    with tc.tile_pool(name="keep", bufs=1) as keep, tc.psum_pool(name="banks", bufs=1) as banks:
+    with tc.tile_pool(name="keep", bufs=1) as keep, tc.psum_pool(
+        name="banks", bufs=1
+    ) as banks, tc.manual_schedule():
         g_rows = keep.tile([P, PASSES, PACK], BF16)
         nc.scalar.dma_start(
             out=g_rows[:], in_=grad_out.rearrange("(c p t) -> p c t", p=P, t=PACK)
@@ -47,34 +47,52 @@ def tile_polynomialtensorregression_pa_v_kernel(
         c_bf16 = keep.tile([P, 3], BF16)
         nc.scalar.dma_start(out=c_bf16[:], in_=C.partition_broadcast(P))
 
+        def load(source, c, first, width, dtype, name):
+            piece = keep.tile([P, PACK, width], dtype, name="%s_%d_%d" % (name, c, first))
+            nc.sync.dma_start(
+                out=piece[:],
+                in_=source[c * K_PASS : (c + 1) * K_PASS, first : first + width].rearrange(
+                    "(p t) w -> p t w", t=PACK
+                ),
+            )
+            return piece
+
         d1, d2, x_raw = [], [], []
         for c in range(PASSES):
-            k_rows = slice(c * K_PASS, (c + 1) * K_PASS)
-            d1.append(keep.tile([P, PACK, R], F32, name="d1_%d" % c))
-            nc.sync.dma_start(
-                out=d1[c][:], in_=dot_2_1[k_rows, :].rearrange("(p t) r -> p t r", t=PACK)
-            )
-            d2.append(keep.tile([P, PACK, R], F32, name="d2_%d" % c))
-            nc.sync.dma_start(
-                out=d2[c][:], in_=dot_2_2[k_rows, :].rearrange("(p t) r -> p t r", t=PACK)
-            )
-            x_raw.append([])
-            for first, width in column_pieces(c):
-                piece = keep.tile([P, PACK, width], BF16, name="x_raw_%d_%d" % (c, first))
-                nc.sync.dma_start(
-                    out=piece[:],
-                    in_=X[k_rows, first : first + width].rearrange("(p t) w -> p t w", t=PACK),
-                )
-                x_raw[c].append(piece)
+            d1.append(load(dot_2_1, c, 0, R, F32, "d1"))
+            d2.append(load(dot_2_2, c, 0, R, F32, "d2"))
+            if c < LAST:
+                x_raw.append(load(X, c, 0, D, BF16, "x_raw"))
+        x_last = [load(X, LAST, first, PIECE, BF16, "x_raw") for first in range(0, D, PIECE)]
 
         c_f32 = keep.tile([P, 3], F32)
         nc.vector.tensor_copy(out=c_f32[:], in_=c_bf16[:])
         row_factor = keep.tile([P, PASSES, PACK], F32)
         nc.vector.tensor_scalar_mul(out=row_factor[:], in0=g_rows[:], scalar1=c_f32[:, 2:3])
 
-        acc = [banks.tile([P, R], F32, name="acc_%d" % m) for m in range(D // M_TILE)]
+        acc = [banks.tile([P, R], F32, name="acc_%d" % m) for m in range(BANKS)]
+        dz_grouped = [
+            keep.tile([P, R, PACK], BF16, name="dz_grouped_%d" % c, align_bytes=64)
+            for c in range(PASSES)
+        ]
+        dz_codes = [
+            keep.tile([P, R], U32, name="dz_codes_%d" % c, align_bytes=64) for c in range(PASSES)
+        ]
+        dz_scales = [
+            keep.tile([P, R], U8, name="dz_scales_%d" % c, align_bytes=64) for c in range(PASSES)
+        ]
+        x_grouped = [
+            keep.tile([P, D, PACK], BF16, name="x_grouped_%d" % c, align_bytes=64)
+            for c in range(PASSES)
+        ]
+        x_codes = [
+            keep.tile([P, D], U32, name="x_codes_%d" % c, align_bytes=64) for c in range(PASSES)
+        ]
+        x_scales = [
+            keep.tile([P, D], U8, name="x_scales_%d" % c, align_bytes=64) for c in range(PASSES)
+        ]
 
-        for c in range(PASSES):
+        def scale_rows(c):
             for t in range(PACK):
                 nc.scalar.activation(
                     out=d1[c][:, t, :],
@@ -82,61 +100,93 @@ def tile_polynomialtensorregression_pa_v_kernel(
                     func=mybir.ActivationFunctionType.Copy,
                     scale=row_factor[:, c, t : t + 1],
                 )
-            dz_grouped = keep.tile([P, R, PACK], BF16, name="dz_grouped_%d" % c, align_bytes=64)
+
+        def multiply_rows(c):
             nc.vector.tensor_tensor(
-                out=grouped_by_runs(dz_grouped[:]),
+                out=grouped_by_runs(dz_grouped[c][:]),
                 in0=rows_by_runs(d1[c][:]),
                 in1=rows_by_runs(d2[c][:]),
                 op=mybir.AluOpType.mult,
             )
-            dz_codes = keep.tile([P, R], U32, name="dz_codes_%d" % c, align_bytes=64)
-            dz_scales = keep.tile([P, R], U8, name="dz_scales_%d" % c, align_bytes=64)
+
+        def quantize_dz(c):
             nc.vector.quantize_mx(
-                out=dz_codes[:].bitcast(E5M2_X4),
-                scales=dz_scales[:],
-                in_=dz_grouped[:].rearrange("p r t -> p (r t)"),
+                out=dz_codes[c][:].bitcast(E5M2_X4),
+                scales=dz_scales[c][:],
+                in_=dz_grouped[c][:].rearrange("p r t -> p (r t)"),
             )
 
-            for piece, (first, width) in zip(x_raw[c], column_pieces(c)):
-                half = width // 2
-                x_grouped = keep.tile(
-                    [P, width, PACK], BF16, name="x_grouped_%d_%d" % (c, first), align_bytes=64
-                )
-                nc.vector.tensor_copy(
-                    out=grouped_by_runs(x_grouped[:, :half, :]),
-                    in_=rows_by_runs(piece[:, :, :half]),
-                )
-                nc.scalar.copy(
-                    out=grouped_by_runs(x_grouped[:, half:, :]),
-                    in_=rows_by_runs(piece[:, :, half:]),
-                )
-                x_codes = keep.tile(
-                    [P, width], U32, name="x_codes_%d_%d" % (c, first), align_bytes=64
-                )
-                x_scales = keep.tile(
-                    [P, width], U8, name="x_scales_%d_%d" % (c, first), align_bytes=64
-                )
-                nc.vector.quantize_mx(
-                    out=x_codes[:].bitcast(E4M3_X4),
-                    scales=x_scales[:],
-                    in_=x_grouped[:].rearrange("p w t -> p (w t)"),
-                )
+        def regroup(engine_copy, c, rows, first, width):
+            engine_copy(
+                out=grouped_by_runs(x_grouped[c][:, first : first + width, :]),
+                in_=rows_by_runs(rows),
+            )
 
-                for local in range(0, width, M_TILE):
-                    m = (first + local) // M_TILE
-                    nc.tensor.matmul_mx(
-                        out=acc[m][:],
-                        lhsT=x_codes[:, local : local + M_TILE].bitcast(E4M3_X4),
-                        lhsT_scale=x_scales[:, local : local + M_TILE],
-                        rhs=dz_codes[:].bitcast(E5M2_X4),
-                        rhs_scale=dz_scales[:],
-                        start=(c == 0),
-                        stop=(c == PASSES - 1),
-                    )
-                    if c == PASSES - 1:
-                        result = keep.tile([P, R], F32, name="result_%d" % m)
-                        if m % 2 == 0:
-                            nc.scalar.copy(out=result[:], in_=acc[m][:])
-                        else:
-                            nc.vector.tensor_copy(out=result[:], in_=acc[m][:])
-                        nc.sync.dma_start(out=out[m * M_TILE : (m + 1) * M_TILE, :], in_=result[:])
+        def quantize_x(c, first, width):
+            cols = slice(first, first + width)
+            nc.vector.quantize_mx(
+                out=x_codes[c][:, cols].bitcast(E4M3_X4),
+                scales=x_scales[c][:, cols],
+                in_=x_grouped[c][:, cols, :].rearrange("p w t -> p (w t)"),
+            )
+
+        def multiply(c, m):
+            cols = slice(m * M_TILE, (m + 1) * M_TILE)
+            nc.tensor.matmul_mx(
+                out=acc[m][:],
+                lhsT=x_codes[c][:, cols].bitcast(E4M3_X4),
+                lhsT_scale=x_scales[c][:, cols],
+                rhs=dz_codes[c][:].bitcast(E5M2_X4),
+                rhs_scale=dz_scales[c][:],
+                start=(c == 0),
+                stop=(c == LAST),
+            )
+
+        def empty_and_store(m):
+            result = keep.tile([P, R], F32, name="result_%d" % m)
+            if m in VECTOR_EMPTIES:
+                nc.vector.tensor_copy(out=result[:], in_=acc[m][:])
+            else:
+                nc.scalar.copy(out=result[:], in_=acc[m][:])
+            nc.sync.dma_start(out=out[m * M_TILE : (m + 1) * M_TILE, :], in_=result[:])
+
+        for c in range(LAST):
+            scale_rows(c)
+            multiply_rows(c)
+            regroup(nc.vector.tensor_copy, c, x_raw[c][:, :, :HALF], 0, HALF)
+            regroup(nc.scalar.copy, c, x_raw[c][:, :, HALF:], HALF, HALF)
+            quantize_dz(c)
+            quantize_x(c, 0, HALF)
+            for m in range(BANKS // 2):
+                multiply(c, m)
+            quantize_x(c, HALF, HALF)
+            for m in range(BANKS // 2, BANKS):
+                multiply(c, m)
+
+        scale_rows(LAST)
+        regroup(nc.scalar.copy, LAST, x_last[0][:], 0, PIECE)
+        regroup(nc.scalar.copy, LAST, x_last[1][:], PIECE, PIECE)
+        multiply_rows(LAST)
+        quantize_x(LAST, 0, PIECE)
+        quantize_dz(LAST)
+        multiply(LAST, 0)
+        multiply(LAST, 1)
+        regroup(nc.vector.tensor_copy, LAST, x_last[2][:], 2 * PIECE, PIECE)
+        empty_and_store(0)
+        quantize_x(LAST, PIECE, PIECE)
+        multiply(LAST, 2)
+        multiply(LAST, 3)
+        regroup(nc.vector.tensor_copy, LAST, x_last[3][:], 3 * PIECE, PIECE)
+        empty_and_store(1)
+        quantize_x(LAST, 2 * PIECE, PIECE)
+        multiply(LAST, 4)
+        multiply(LAST, 5)
+        empty_and_store(2)
+        quantize_x(LAST, 3 * PIECE, PIECE)
+        multiply(LAST, 6)
+        multiply(LAST, 7)
+        empty_and_store(3)
+        empty_and_store(5)
+        empty_and_store(4)
+        empty_and_store(7)
+        empty_and_store(6)

@@ -63,7 +63,11 @@ def tile_polynomialtensorregression_pa_v_kernel(
             d2.append(load(dot_2_2, c, 0, R, F32, "d2"))
             if c < LAST:
                 x_raw.append(load(X, c, 0, D, BF16, "x_raw"))
-        x_last = [load(X, LAST, first, PIECE, BF16, "x_raw") for first in range(0, D, PIECE)]
+        x_halves = [load(X, LAST, first, HALF, BF16, "x_raw") for first in (0, HALF)]
+        x_last = [
+            x_halves[first // HALF][:, :, first % HALF : first % HALF + PIECE]
+            for first in range(0, D, PIECE)
+        ]
 
         c_f32 = keep.tile([P, 3], F32)
         nc.vector.tensor_copy(out=c_f32[:], in_=c_bf16[:])
@@ -163,20 +167,30 @@ def tile_polynomialtensorregression_pa_v_kernel(
             for m in range(BANKS // 2, BANKS):
                 multiply(c, m)
 
-        scale_rows(LAST)
-        regroup(nc.scalar.copy, LAST, x_last[0][:], 0, PIECE)
-        regroup(nc.scalar.copy, LAST, x_last[1][:], PIECE, PIECE)
+        for t in (0, 1):
+            nc.scalar.activation(
+                out=d1[LAST][:, t, :],
+                in_=d1[LAST][:, t, :],
+                func=mybir.ActivationFunctionType.Copy,
+                scale=row_factor[:, LAST, t : t + 1],
+            )
+        for t in (2, 3):
+            nc.vector.tensor_scalar_mul(
+                out=d1[LAST][:, t, :], in0=d1[LAST][:, t, :], scalar1=row_factor[:, LAST, t : t + 1]
+            )
+        regroup(nc.scalar.copy, LAST, x_last[0], 0, PIECE)
+        regroup(nc.scalar.copy, LAST, x_last[1], PIECE, PIECE)
         multiply_rows(LAST)
         quantize_x(LAST, 0, PIECE)
         quantize_dz(LAST)
         multiply(LAST, 0)
         multiply(LAST, 1)
-        regroup(nc.vector.tensor_copy, LAST, x_last[2][:], 2 * PIECE, PIECE)
+        regroup(nc.vector.tensor_copy, LAST, x_last[2], 2 * PIECE, PIECE)
         empty_and_store(0)
         quantize_x(LAST, PIECE, PIECE)
         multiply(LAST, 2)
         multiply(LAST, 3)
-        regroup(nc.vector.tensor_copy, LAST, x_last[3][:], 3 * PIECE, PIECE)
+        regroup(nc.vector.tensor_copy, LAST, x_last[3], 3 * PIECE, PIECE)
         empty_and_store(1)
         quantize_x(LAST, 2 * PIECE, PIECE)
         multiply(LAST, 4)

@@ -16,6 +16,7 @@ LAST = PASSES - 1
 M_TILE = 128
 BANKS = D // M_TILE
 RUN = 4
+X_RUN = 8
 PIECE = 256
 HALF = D // 2
 
@@ -122,8 +123,10 @@ def tile_polynomialtensorregression_pa_v_kernel(
 
         def regroup(engine_copy, c, rows, first, width):
             engine_copy(
-                out=grouped_by_runs(x_grouped[c][:, first : first + width, :]),
-                in_=rows_by_runs(rows),
+                out=x_grouped[c][:, first : first + width, :].rearrange(
+                    "p (g i) t -> p g t i", i=X_RUN
+                ),
+                in_=rows.rearrange("p t (g i) -> p g t i", i=X_RUN),
             )
 
         def quantize_x(c, first, width):

@@ -15,23 +15,25 @@ PASSES = B // K_PASS
 LAST = PASSES - 1
 M_TILE = 128
 BANKS = D // M_TILE
-RUN = 4
-X_RUN = 8
-PIECE = 256
 HALF = D // 2
+
+DZ_RUN = 4
+X_RUN = 8
+
+PIECE = 2 * M_TILE
+PIECES = D // PIECE
+SCALAR_PIECES = 2
 
 FLOPS = 2 * B * D * R
 BYTES = 2 * B * D + 2 * 4 * B * R + 2 * B + 2 + 4 * D * R
 
-VECTOR_EMPTIES = (5, 7)
+
+def rows_by_runs(rows, run):
+    return rows.rearrange("p t (g i) -> p g t i", i=run)
 
 
-def rows_by_runs(rows):
-    return rows.rearrange("p t (g i) -> p g t i", i=RUN)
-
-
-def grouped_by_runs(grouped):
-    return grouped.rearrange("p (g i) t -> p g t i", i=RUN)
+def grouped_by_runs(grouped, run):
+    return grouped.rearrange("p (g i) t -> p g t i", i=run)
 
 
 def tile_polynomialtensorregression_pa_v_kernel(
@@ -45,8 +47,11 @@ def tile_polynomialtensorregression_pa_v_kernel(
         nc.scalar.dma_start(
             out=g_rows[:], in_=grad_out.rearrange("(c p t) -> p c t", p=P, t=PACK)
         )
-        c_bf16 = keep.tile([P, 3], BF16)
-        nc.scalar.dma_start(out=c_bf16[:], in_=C.partition_broadcast(P))
+        ones = keep.tile([P, P], BF16)
+        nc.vector.memset(ones[:], 1.0)
+        c_row = keep.tile([P, 4], BF16)
+        nc.vector.memset(c_row[:], 0.0)
+        nc.scalar.dma_start(out=c_row[0:1, 0:3], in_=C.rearrange("(o n) -> o n", o=1))
 
         def load(source, c, first, width, dtype, name):
             piece = keep.tile([P, PACK, width], dtype, name="%s_%d_%d" % (name, c, first))
@@ -64,18 +69,17 @@ def tile_polynomialtensorregression_pa_v_kernel(
             d2.append(load(dot_2_2, c, 0, R, F32, "d2"))
             if c < LAST:
                 x_raw.append(load(X, c, 0, D, BF16, "x_raw"))
-        x_halves = [load(X, LAST, first, HALF, BF16, "x_raw") for first in (0, HALF)]
-        x_last = [
-            x_halves[first // HALF][:, :, first % HALF : first % HALF + PIECE]
-            for first in range(0, D, PIECE)
-        ]
+        x_last = [load(X, LAST, first, HALF, BF16, "x_raw") for first in (0, HALF)]
 
-        c_f32 = keep.tile([P, 3], F32)
-        nc.vector.tensor_copy(out=c_f32[:], in_=c_bf16[:])
+        acc = [banks.tile([P, R], F32, name="acc_%d" % m) for m in range(BANKS)]
+        nc.tensor.matmul(
+            out=acc[BANKS - 1][:, 0:4], lhsT=ones[:], rhs=c_row[:], start=True, stop=True
+        )
+        c_f32 = keep.tile([P, 4], F32)
+        nc.vector.tensor_copy(out=c_f32[:], in_=acc[BANKS - 1][:, 0:4])
         row_factor = keep.tile([P, PASSES, PACK], F32)
         nc.vector.tensor_scalar_mul(out=row_factor[:], in0=g_rows[:], scalar1=c_f32[:, 2:3])
 
-        acc = [banks.tile([P, R], F32, name="acc_%d" % m) for m in range(BANKS)]
         dz_grouped = [
             keep.tile([P, R, PACK], BF16, name="dz_grouped_%d" % c, align_bytes=64)
             for c in range(PASSES)
@@ -97,20 +101,24 @@ def tile_polynomialtensorregression_pa_v_kernel(
             keep.tile([P, D], U8, name="x_scales_%d" % c, align_bytes=64) for c in range(PASSES)
         ]
 
-        def scale_rows(c):
-            for t in range(PACK):
-                nc.scalar.activation(
-                    out=d1[c][:, t, :],
-                    in_=d1[c][:, t, :],
-                    func=mybir.ActivationFunctionType.Copy,
-                    scale=row_factor[:, c, t : t + 1],
-                )
+        def scale_row_on_scalar(c, t):
+            nc.scalar.activation(
+                out=d1[c][:, t, :],
+                in_=d1[c][:, t, :],
+                func=mybir.ActivationFunctionType.Copy,
+                scale=row_factor[:, c, t : t + 1],
+            )
+
+        def scale_row_on_vector(c, t):
+            nc.vector.tensor_scalar_mul(
+                out=d1[c][:, t, :], in0=d1[c][:, t, :], scalar1=row_factor[:, c, t : t + 1]
+            )
 
         def multiply_rows(c):
             nc.vector.tensor_tensor(
-                out=grouped_by_runs(dz_grouped[c][:]),
-                in0=rows_by_runs(d1[c][:]),
-                in1=rows_by_runs(d2[c][:]),
+                out=grouped_by_runs(dz_grouped[c][:], DZ_RUN),
+                in0=rows_by_runs(d1[c][:], DZ_RUN),
+                in1=rows_by_runs(d2[c][:], DZ_RUN),
                 op=mybir.AluOpType.mult,
             )
 
@@ -123,11 +131,14 @@ def tile_polynomialtensorregression_pa_v_kernel(
 
         def regroup(engine_copy, c, rows, first, width):
             engine_copy(
-                out=x_grouped[c][:, first : first + width, :].rearrange(
-                    "p (g i) t -> p g t i", i=X_RUN
-                ),
-                in_=rows.rearrange("p t (g i) -> p g t i", i=X_RUN),
+                out=grouped_by_runs(x_grouped[c][:, first : first + width, :], X_RUN),
+                in_=rows_by_runs(rows, X_RUN),
             )
+
+        def regroup_piece(engine_copy, i):
+            first = i * PIECE
+            rows = x_last[first // HALF][:, :, first % HALF : first % HALF + PIECE]
+            regroup(engine_copy, LAST, rows, first, PIECE)
 
         def quantize_x(c, first, width):
             cols = slice(first, first + width)
@@ -149,61 +160,39 @@ def tile_polynomialtensorregression_pa_v_kernel(
                 stop=(c == LAST),
             )
 
-        def empty_and_store(m):
+        def empty_and_store(engine_copy, m):
             result = keep.tile([P, R], F32, name="result_%d" % m)
-            if m in VECTOR_EMPTIES:
-                nc.vector.tensor_copy(out=result[:], in_=acc[m][:])
-            else:
-                nc.scalar.copy(out=result[:], in_=acc[m][:])
+            engine_copy(out=result[:], in_=acc[m][:])
             nc.sync.dma_start(out=out[m * M_TILE : (m + 1) * M_TILE, :], in_=result[:])
 
         for c in range(LAST):
-            scale_rows(c)
+            for t in range(PACK):
+                scale_row_on_scalar(c, t)
             multiply_rows(c)
             regroup(nc.vector.tensor_copy, c, x_raw[c][:, :, :HALF], 0, HALF)
             regroup(nc.scalar.copy, c, x_raw[c][:, :, HALF:], HALF, HALF)
             quantize_dz(c)
-            quantize_x(c, 0, HALF)
-            for m in range(BANKS // 2):
-                multiply(c, m)
-            quantize_x(c, HALF, HALF)
-            for m in range(BANKS // 2, BANKS):
-                multiply(c, m)
+            for first in (0, HALF):
+                quantize_x(c, first, HALF)
+                for m in range(first // M_TILE, (first + HALF) // M_TILE):
+                    multiply(c, m)
 
-        for t in (0, 1):
-            nc.scalar.activation(
-                out=d1[LAST][:, t, :],
-                in_=d1[LAST][:, t, :],
-                func=mybir.ActivationFunctionType.Copy,
-                scale=row_factor[:, LAST, t : t + 1],
-            )
-        for t in (2, 3):
-            nc.vector.tensor_scalar_mul(
-                out=d1[LAST][:, t, :], in0=d1[LAST][:, t, :], scalar1=row_factor[:, LAST, t : t + 1]
-            )
-        regroup(nc.scalar.copy, LAST, x_last[0], 0, PIECE)
-        regroup(nc.scalar.copy, LAST, x_last[1], PIECE, PIECE)
+        for t in range(PACK // 2):
+            scale_row_on_scalar(LAST, t)
+        for t in range(PACK // 2, PACK):
+            scale_row_on_vector(LAST, t)
+        for i in range(SCALAR_PIECES):
+            regroup_piece(nc.scalar.copy, i)
         multiply_rows(LAST)
-        quantize_x(LAST, 0, PIECE)
-        quantize_dz(LAST)
-        multiply(LAST, 0)
-        multiply(LAST, 1)
-        regroup(nc.vector.tensor_copy, LAST, x_last[2], 2 * PIECE, PIECE)
-        empty_and_store(0)
-        quantize_x(LAST, PIECE, PIECE)
-        multiply(LAST, 2)
-        multiply(LAST, 3)
-        regroup(nc.vector.tensor_copy, LAST, x_last[3], 3 * PIECE, PIECE)
-        empty_and_store(1)
-        quantize_x(LAST, 2 * PIECE, PIECE)
-        multiply(LAST, 4)
-        multiply(LAST, 5)
-        empty_and_store(2)
-        quantize_x(LAST, 3 * PIECE, PIECE)
-        multiply(LAST, 6)
-        multiply(LAST, 7)
-        empty_and_store(3)
-        empty_and_store(5)
-        empty_and_store(4)
-        empty_and_store(7)
-        empty_and_store(6)
+        for i in range(PIECES):
+            quantize_x(LAST, i * PIECE, PIECE)
+            if i == 0:
+                quantize_dz(LAST)
+            multiply(LAST, 2 * i)
+            multiply(LAST, 2 * i + 1)
+            if i + SCALAR_PIECES < PIECES:
+                regroup_piece(nc.vector.tensor_copy, i + SCALAR_PIECES)
+            empty_and_store(nc.scalar.copy, i)
+        for m in range(PIECES, BANKS, 2):
+            empty_and_store(nc.vector.tensor_copy, m + 1)
+            empty_and_store(nc.scalar.copy, m)

@@ -1,4 +1,5 @@
 import concourse.mybir as mybir
+from concourse.masks import make_identity
 
 BF16 = mybir.dt.bfloat16
 F32 = mybir.dt.float32
@@ -43,15 +44,10 @@ def tile_polynomialtensorregression_pa_v_kernel(
     with tc.tile_pool(name="keep", bufs=1) as keep, tc.psum_pool(
         name="banks", bufs=1
     ) as banks, tc.manual_schedule():
-        g_rows = keep.tile([P, PASSES, PACK], BF16)
-        nc.scalar.dma_start(
-            out=g_rows[:], in_=grad_out.rearrange("(c p t) -> p c t", p=P, t=PACK)
-        )
-        ones = keep.tile([P, P], BF16)
-        nc.vector.memset(ones[:], 1.0)
-        c_row = keep.tile([P, 4], BF16)
-        nc.vector.memset(c_row[:], 0.0)
-        nc.scalar.dma_start(out=c_row[0:1, 0:3], in_=C.rearrange("(o n) -> o n", o=1))
+        g_in = keep.tile([PASSES, K_PASS], BF16)
+        nc.scalar.dma_start(out=g_in[:], in_=grad_out.rearrange("(c k) -> c k", k=K_PASS))
+        c_in = keep.tile([1, 3], BF16)
+        nc.scalar.dma_start(out=c_in[:], in_=C.rearrange("(o n) -> o n", o=1))
 
         def load(source, c, first, width, dtype, name):
             piece = keep.tile([P, PACK, width], dtype, name="%s_%d_%d" % (name, c, first))
@@ -72,13 +68,34 @@ def tile_polynomialtensorregression_pa_v_kernel(
         x_last = [load(X, LAST, first, HALF, BF16, "x_raw") for first in (0, HALF)]
 
         acc = [banks.tile([P, R], F32, name="acc_%d" % m) for m in range(BANKS)]
-        nc.tensor.matmul(
-            out=acc[BANKS - 1][:, 0:4], lhsT=ones[:], rhs=c_row[:], start=True, stop=True
-        )
+        ident = keep.tile([P, P], BF16)
+        make_identity(nc, ident[:])
+        ones = keep.tile([P, P], BF16)
+        nc.vector.memset(ones[:], 1.0)
+        c_row = keep.tile([P, 4], BF16)
+        nc.vector.memset(c_row[:], 0.0)
+        g_stage = keep.tile([P, K_PASS], BF16)
+        nc.vector.memset(g_stage[:], 0.0)
+        nc.vector.tensor_copy(out=c_row[0:1, 0:3], in_=c_in[:])
+        nc.vector.tensor_copy(out=g_stage[0:PASSES, :], in_=g_in[:])
+        borrowed = acc[BANKS - 1]
+        nc.tensor.matmul(out=borrowed[:, 0:4], lhsT=ones[:], rhs=c_row[:], start=True, stop=True)
+        for t in range(PACK):
+            nc.tensor.matmul(
+                out=borrowed[:, 4 + PASSES * t : 4 + PASSES * (t + 1)],
+                lhsT=g_stage[:, t::PACK],
+                rhs=ident[:, 0:PASSES],
+                start=True,
+                stop=True,
+            )
         c_f32 = keep.tile([P, 4], F32)
-        nc.vector.tensor_copy(out=c_f32[:], in_=acc[BANKS - 1][:, 0:4])
+        nc.vector.tensor_copy(out=c_f32[:], in_=borrowed[:, 0:4])
         row_factor = keep.tile([P, PASSES, PACK], F32)
-        nc.vector.tensor_scalar_mul(out=row_factor[:], in0=g_rows[:], scalar1=c_f32[:, 2:3])
+        nc.vector.tensor_scalar_mul(
+            out=row_factor[:].rearrange("p c t -> p t c"),
+            in0=borrowed[:, 4 : 4 + PASSES * PACK].rearrange("p (t c) -> p t c", t=PACK),
+            scalar1=c_f32[:, 2:3],
+        )
 
         dz_grouped = [
             keep.tile([P, R, PACK], BF16, name="dz_grouped_%d" % c, align_bytes=64)

@@ -44,11 +44,6 @@ def tile_polynomialtensorregression_pa_v_kernel(
     with tc.tile_pool(name="keep", bufs=1) as keep, tc.psum_pool(
         name="banks", bufs=1
     ) as banks, tc.manual_schedule():
-        g_in = keep.tile([PASSES, K_PASS], BF16)
-        nc.scalar.dma_start(out=g_in[:], in_=grad_out.rearrange("(c k) -> c k", k=K_PASS))
-        c_in = keep.tile([1, 3], BF16)
-        nc.scalar.dma_start(out=c_in[:], in_=C.rearrange("(o n) -> o n", o=1))
-
         def load(source, c, first, width, dtype, name):
             piece = keep.tile([P, PACK, width], dtype, name="%s_%d_%d" % (name, c, first))
             nc.sync.dma_start(
@@ -60,42 +55,47 @@ def tile_polynomialtensorregression_pa_v_kernel(
             return piece
 
         d1, d2, x_raw = [], [], []
+        g_in = keep.tile([PASSES, K_PASS], BF16)
+        c_in = keep.tile([PASSES, 3], BF16)
         for c in range(PASSES):
-            d1.append(load(dot_2_1, c, 0, R, F32, "d1"))
-            d2.append(load(dot_2_2, c, 0, R, F32, "d2"))
             if c < LAST:
                 x_raw.append(load(X, c, 0, D, BF16, "x_raw"))
+            if c == 0:
+                nc.sync.dma_start(out=g_in[:], in_=grad_out.rearrange("(c k) -> c k", k=K_PASS))
+                nc.sync.dma_start(out=c_in[:], in_=C.partition_broadcast(PASSES))
+            d1.append(load(dot_2_1, c, 0, R, F32, "d1"))
+            d2.append(load(dot_2_2, c, 0, R, F32, "d2"))
         x_last = [load(X, LAST, first, HALF, BF16, "x_raw") for first in (0, HALF)]
 
         acc = [banks.tile([P, R], F32, name="acc_%d" % m) for m in range(BANKS)]
         ident = keep.tile([P, P], BF16)
         make_identity(nc, ident[:])
-        ones = keep.tile([P, P], BF16)
-        nc.vector.memset(ones[:], 1.0)
-        c_row = keep.tile([P, 4], BF16)
-        nc.vector.memset(c_row[:], 0.0)
+        c_diag = keep.tile([P, PASSES], BF16)
+        nc.vector.memset(c_diag[:], 0.0)
         g_stage = keep.tile([P, K_PASS], BF16)
         nc.vector.memset(g_stage[:], 0.0)
-        nc.vector.tensor_copy(out=c_row[0:1, 0:3], in_=c_in[:])
-        nc.vector.tensor_copy(out=g_stage[0:PASSES, :], in_=g_in[:])
         borrowed = acc[BANKS - 1]
-        nc.tensor.matmul(out=borrowed[:, 0:4], lhsT=ones[:], rhs=c_row[:], start=True, stop=True)
-        for t in range(PACK):
-            nc.tensor.matmul(
-                out=borrowed[:, 4 + PASSES * t : 4 + PASSES * (t + 1)],
-                lhsT=g_stage[:, t::PACK],
-                rhs=ident[:, 0:PASSES],
-                start=True,
-                stop=True,
+        row_factor = keep.tile([P, PACK, PASSES], F32)
+
+        def stage_row_factors():
+            nc.vector.tensor_copy(out=g_stage[0:PASSES, :], in_=g_in[:])
+            nc.vector.tensor_scalar_mul(
+                out=c_diag[0:PASSES, :], in0=ident[0:PASSES, 0:PASSES], scalar1=c_in[:, 2:3]
             )
-        c_f32 = keep.tile([P, 4], F32)
-        nc.vector.tensor_copy(out=c_f32[:], in_=borrowed[:, 0:4])
-        row_factor = keep.tile([P, PASSES, PACK], F32)
-        nc.vector.tensor_scalar_mul(
-            out=row_factor[:].rearrange("p c t -> p t c"),
-            in0=borrowed[:, 4 : 4 + PASSES * PACK].rearrange("p (t c) -> p t c", t=PACK),
-            scalar1=c_f32[:, 2:3],
-        )
+            for t in range(PACK):
+                nc.tensor.matmul(
+                    out=borrowed[:, PASSES * t : PASSES * (t + 1)],
+                    lhsT=g_stage[:, t::PACK],
+                    rhs=c_diag[:],
+                    start=True,
+                    stop=True,
+                )
+
+        def fetch_row_factors():
+            nc.vector.tensor_copy(
+                out=row_factor[:].rearrange("p t c -> p (t c)"),
+                in_=borrowed[:, 0 : PACK * PASSES],
+            )
 
         dz_grouped = [
             keep.tile([P, R, PACK], BF16, name="dz_grouped_%d" % c, align_bytes=64)
@@ -123,12 +123,12 @@ def tile_polynomialtensorregression_pa_v_kernel(
                 out=d1[c][:, t, :],
                 in_=d1[c][:, t, :],
                 func=mybir.ActivationFunctionType.Copy,
-                scale=row_factor[:, c, t : t + 1],
+                scale=row_factor[:, t, c : c + 1],
             )
 
         def scale_row_on_vector(c, t):
             nc.vector.tensor_scalar_mul(
-                out=d1[c][:, t, :], in0=d1[c][:, t, :], scalar1=row_factor[:, c, t : t + 1]
+                out=d1[c][:, t, :], in0=d1[c][:, t, :], scalar1=row_factor[:, t, c : c + 1]
             )
 
         def multiply_rows(c):
@@ -182,22 +182,33 @@ def tile_polynomialtensorregression_pa_v_kernel(
             engine_copy(out=result[:], in_=acc[m][:])
             nc.sync.dma_start(out=out[m * M_TILE : (m + 1) * M_TILE, :], in_=result[:])
 
-        for c in range(LAST):
-            for t in range(PACK):
+        def scale(c):
+            for t in range(PACK // 2):
                 scale_row_on_scalar(c, t)
-            multiply_rows(c)
+            for t in range(PACK // 2, PACK):
+                scale_row_on_vector(c, t)
+
+        def finish(c):
+            quantize_dz(c)
+            for m in range(BANKS):
+                multiply(c, m)
+
+        for c in range(LAST):
             regroup(nc.vector.tensor_copy, c, x_raw[c][:, :, :HALF], 0, HALF)
             regroup(nc.scalar.copy, c, x_raw[c][:, :, HALF:], HALF, HALF)
-            quantize_dz(c)
-            for first in (0, HALF):
-                quantize_x(c, first, HALF)
-                for m in range(first // M_TILE, (first + HALF) // M_TILE):
-                    multiply(c, m)
+            if c == 0:
+                stage_row_factors()
+            else:
+                finish(c - 1)
+            quantize_x(c, 0, HALF)
+            if c == 0:
+                fetch_row_factors()
+            quantize_x(c, HALF, HALF)
+            scale(c)
+            multiply_rows(c)
+        finish(LAST - 1)
 
-        for t in range(PACK // 2):
-            scale_row_on_scalar(LAST, t)
-        for t in range(PACK // 2, PACK):
-            scale_row_on_vector(LAST, t)
+        scale(LAST)
         for i in range(SCALAR_PIECES):
             regroup_piece(nc.scalar.copy, i)
         multiply_rows(LAST)

@@ -21,10 +21,6 @@ HALF = D // 2
 DZ_RUN = 4
 X_RUN = 8
 
-PIECE = 2 * M_TILE
-PIECES = D // PIECE
-SCALAR_PIECES = 2
-
 FLOPS = 2 * B * D * R
 BYTES = 2 * B * D + 2 * 4 * B * R + 2 * B + 2 + 4 * D * R
 
@@ -131,19 +127,21 @@ def tile_polynomialtensorregression_pa_v_kernel(
                 out=d1[c][:, t, :], in0=d1[c][:, t, :], scalar1=row_factor[:, t, c : c + 1]
             )
 
-        def multiply_rows(c):
+        def multiply_rows(c, first=0, width=R):
+            cols = slice(first, first + width)
             nc.vector.tensor_tensor(
-                out=grouped_by_runs(dz_grouped[c][:], DZ_RUN),
-                in0=rows_by_runs(d1[c][:], DZ_RUN),
-                in1=rows_by_runs(d2[c][:], DZ_RUN),
+                out=grouped_by_runs(dz_grouped[c][:, cols, :], DZ_RUN),
+                in0=rows_by_runs(d1[c][:, :, cols], DZ_RUN),
+                in1=rows_by_runs(d2[c][:, :, cols], DZ_RUN),
                 op=mybir.AluOpType.mult,
             )
 
-        def quantize_dz(c):
+        def quantize_dz(c, first=0, width=R):
+            cols = slice(first, first + width)
             nc.vector.quantize_mx(
-                out=dz_codes[c][:].bitcast(E5M2_X4),
-                scales=dz_scales[c][:],
-                in_=dz_grouped[c][:].rearrange("p r t -> p (r t)"),
+                out=dz_codes[c][:, cols].bitcast(E5M2_X4),
+                scales=dz_scales[c][:, cols],
+                in_=dz_grouped[c][:, cols, :].rearrange("p r t -> p (r t)"),
             )
 
         def regroup(engine_copy, c, rows, first, width):
@@ -152,10 +150,15 @@ def tile_polynomialtensorregression_pa_v_kernel(
                 in_=rows_by_runs(rows, X_RUN),
             )
 
-        def regroup_piece(engine_copy, i):
-            first = i * PIECE
-            rows = x_last[first // HALF][:, :, first % HALF : first % HALF + PIECE]
-            regroup(engine_copy, LAST, rows, first, PIECE)
+        def regroup_last(engine_copy, m, banks_wide):
+            first, width = m * M_TILE, banks_wide * M_TILE
+            rows = x_last[first // HALF][:, :, first % HALF : first % HALF + width]
+            regroup(engine_copy, LAST, rows, first, width)
+
+        def quantize_last(m, banks_wide):
+            quantize_x(LAST, m * M_TILE, banks_wide * M_TILE)
+            for k in range(m, m + banks_wide):
+                multiply(LAST, k)
 
         def quantize_x(c, first, width):
             cols = slice(first, first + width)
@@ -209,18 +212,26 @@ def tile_polynomialtensorregression_pa_v_kernel(
         finish(LAST - 1)
 
         scale(LAST)
-        for i in range(SCALAR_PIECES):
-            regroup_piece(nc.scalar.copy, i)
-        multiply_rows(LAST)
-        for i in range(PIECES):
-            quantize_x(LAST, i * PIECE, PIECE)
-            if i == 0:
-                quantize_dz(LAST)
-            multiply(LAST, 2 * i)
-            multiply(LAST, 2 * i + 1)
-            if i + SCALAR_PIECES < PIECES:
-                regroup_piece(nc.vector.tensor_copy, i + SCALAR_PIECES)
-            empty_and_store(nc.scalar.copy, i)
-        for m in range(PIECES, BANKS, 2):
+        for m in range(3):
+            regroup_last(nc.scalar.copy, m, 1)
+        for first in (0, R // 2):
+            multiply_rows(LAST, first, R // 2)
+        for first in (0, R // 2):
+            quantize_dz(LAST, first, R // 2)
+        quantize_last(0, 1)
+        quantize_last(1, 1)
+        regroup_last(nc.vector.tensor_copy, 3, 1)
+        empty_and_store(nc.scalar.copy, 0)
+        quantize_last(2, 1)
+        quantize_last(3, 1)
+        empty_and_store(nc.scalar.copy, 1)
+        regroup_last(nc.vector.tensor_copy, 4, 2)
+        empty_and_store(nc.scalar.copy, 2)
+        regroup_last(nc.vector.tensor_copy, 6, 1)
+        quantize_last(4, 2)
+        empty_and_store(nc.scalar.copy, 3)
+        regroup_last(nc.vector.tensor_copy, 7, 1)
+        quantize_last(6, 2)
+        for m in (4, 6):
             empty_and_store(nc.vector.tensor_copy, m + 1)
             empty_and_store(nc.scalar.copy, m)

@@ -17,6 +17,7 @@ LAST = PASSES - 1
 M_TILE = 128
 BANKS = D // M_TILE
 HALF = D // 2
+LAST_X_LOADS = ((0, HALF // 2), (HALF // 2, HALF // 2), (HALF, HALF))
 
 DZ_RUN = 4
 X_RUN = 8
@@ -60,8 +61,13 @@ def tile_polynomialtensorregression_pa_v_kernel(
                 nc.sync.dma_start(out=g_in[:], in_=grad_out.rearrange("(c k) -> c k", k=K_PASS))
                 nc.sync.dma_start(out=c_in[:], in_=C.partition_broadcast(PASSES))
             d1.append(load(dot_2_1, c, 0, R, F32, "d1"))
-            d2.append(load(dot_2_2, c, 0, R, F32, "d2"))
-        x_last = [load(X, LAST, first, HALF, BF16, "x_raw") for first in (0, HALF)]
+            if c < LAST:
+                d2.append(load(dot_2_2, c, 0, R, F32, "d2"))
+        d2_last = [load(dot_2_2, LAST, first, R // 2, F32, "d2") for first in (0, R // 2)]
+        x_last = [
+            (first, width, load(X, LAST, first, width, BF16, "x_raw"))
+            for first, width in LAST_X_LOADS
+        ]
 
         acc = [banks.tile([P, R], F32, name="acc_%d" % m) for m in range(BANKS)]
         ident = keep.tile([P, P], BF16)
@@ -127,12 +133,12 @@ def tile_polynomialtensorregression_pa_v_kernel(
                 out=d1[c][:, t, :], in0=d1[c][:, t, :], scalar1=row_factor[:, t, c : c + 1]
             )
 
-        def multiply_rows(c, first=0, width=R):
+        def multiply_rows(c, factor, first=0, width=R):
             cols = slice(first, first + width)
             nc.vector.tensor_tensor(
                 out=grouped_by_runs(dz_grouped[c][:, cols, :], DZ_RUN),
                 in0=rows_by_runs(d1[c][:, :, cols], DZ_RUN),
-                in1=rows_by_runs(d2[c][:, :, cols], DZ_RUN),
+                in1=rows_by_runs(factor[:], DZ_RUN),
                 op=mybir.AluOpType.mult,
             )
 
@@ -152,8 +158,10 @@ def tile_polynomialtensorregression_pa_v_kernel(
 
         def regroup_last(engine_copy, m, banks_wide):
             first, width = m * M_TILE, banks_wide * M_TILE
-            rows = x_last[first // HALF][:, :, first % HALF : first % HALF + width]
-            regroup(engine_copy, LAST, rows, first, width)
+            for left, loaded, piece in x_last:
+                if left <= first and first + width <= left + loaded:
+                    rows = piece[:, :, first - left : first - left + width]
+                    regroup(engine_copy, LAST, rows, first, width)
 
         def quantize_last(m, banks_wide):
             quantize_x(LAST, m * M_TILE, banks_wide * M_TILE)
@@ -208,30 +216,31 @@ def tile_polynomialtensorregression_pa_v_kernel(
                 fetch_row_factors()
             quantize_x(c, HALF, HALF)
             scale(c)
-            multiply_rows(c)
-        finish(LAST - 1)
+            multiply_rows(c, d2[c])
 
         scale(LAST)
-        for m in range(3):
-            regroup_last(nc.scalar.copy, m, 1)
-        for first in (0, R // 2):
-            multiply_rows(LAST, first, R // 2)
+        finish(LAST - 1)
+        regroup_last(nc.scalar.copy, 0, 2)
+        regroup_last(nc.scalar.copy, 2, 1)
+        for first, factor in zip((0, R // 2), d2_last):
+            multiply_rows(LAST, factor, first, R // 2)
         for first in (0, R // 2):
             quantize_dz(LAST, first, R // 2)
         quantize_last(0, 1)
         quantize_last(1, 1)
-        regroup_last(nc.vector.tensor_copy, 3, 1)
         empty_and_store(nc.scalar.copy, 0)
+        regroup_last(nc.vector.tensor_copy, 3, 1)
         quantize_last(2, 1)
-        quantize_last(3, 1)
         empty_and_store(nc.scalar.copy, 1)
-        regroup_last(nc.vector.tensor_copy, 4, 2)
+        quantize_last(3, 1)
         empty_and_store(nc.scalar.copy, 2)
+        regroup_last(nc.vector.tensor_copy, 4, 2)
+        empty_and_store(nc.scalar.copy, 3)
         regroup_last(nc.vector.tensor_copy, 6, 1)
         quantize_last(4, 2)
-        empty_and_store(nc.scalar.copy, 3)
+        empty_and_store(nc.scalar.copy, 4)
         regroup_last(nc.vector.tensor_copy, 7, 1)
+        empty_and_store(nc.scalar.copy, 5)
         quantize_last(6, 2)
-        for m in (4, 6):
-            empty_and_store(nc.vector.tensor_copy, m + 1)
-            empty_and_store(nc.scalar.copy, m)
+        empty_and_store(nc.scalar.copy, 6)
+        empty_and_store(nc.vector.tensor_copy, 7)

@@ -17,6 +17,7 @@ LAST = PASSES - 1
 M_TILE = 128
 BANKS = D // M_TILE
 HALF = D // 2
+AHEAD = 2
 LAST_X_LOADS = ((0, HALF // 2), (HALF // 2, HALF // 2), (HALF, HALF))
 
 DZ_RUN = 4
@@ -156,17 +157,12 @@ def tile_polynomialtensorregression_pa_v_kernel(
                 in_=rows_by_runs(rows, X_RUN),
             )
 
-        def regroup_last(engine_copy, m, banks_wide):
-            first, width = m * M_TILE, banks_wide * M_TILE
+        def regroup_last(engine_copy, m):
+            first = m * M_TILE
             for left, loaded, piece in x_last:
-                if left <= first and first + width <= left + loaded:
-                    rows = piece[:, :, first - left : first - left + width]
-                    regroup(engine_copy, LAST, rows, first, width)
-
-        def quantize_last(m, banks_wide):
-            quantize_x(LAST, m * M_TILE, banks_wide * M_TILE)
-            for k in range(m, m + banks_wide):
-                multiply(LAST, k)
+                if left <= first < left + loaded:
+                    rows = piece[:, :, first - left : first - left + M_TILE]
+                    regroup(engine_copy, LAST, rows, first, M_TILE)
 
         def quantize_x(c, first, width):
             cols = slice(first, first + width)
@@ -220,27 +216,15 @@ def tile_polynomialtensorregression_pa_v_kernel(
 
         scale(LAST)
         finish(LAST - 1)
-        regroup_last(nc.scalar.copy, 0, 2)
-        regroup_last(nc.scalar.copy, 2, 1)
+        for m in range(AHEAD):
+            regroup_last(nc.scalar.copy, m)
         for first, factor in zip((0, R // 2), d2_last):
             multiply_rows(LAST, factor, first, R // 2)
         for first in (0, R // 2):
             quantize_dz(LAST, first, R // 2)
-        quantize_last(0, 1)
-        quantize_last(1, 1)
-        empty_and_store(nc.scalar.copy, 0)
-        regroup_last(nc.vector.tensor_copy, 3, 1)
-        quantize_last(2, 1)
-        empty_and_store(nc.scalar.copy, 1)
-        quantize_last(3, 1)
-        empty_and_store(nc.scalar.copy, 2)
-        regroup_last(nc.vector.tensor_copy, 4, 2)
-        empty_and_store(nc.scalar.copy, 3)
-        regroup_last(nc.vector.tensor_copy, 6, 1)
-        quantize_last(4, 2)
-        empty_and_store(nc.scalar.copy, 4)
-        regroup_last(nc.vector.tensor_copy, 7, 1)
-        empty_and_store(nc.scalar.copy, 5)
-        quantize_last(6, 2)
-        empty_and_store(nc.scalar.copy, 6)
-        empty_and_store(nc.vector.tensor_copy, 7)
+        for m in range(BANKS):
+            quantize_x(LAST, m * M_TILE, M_TILE)
+            multiply(LAST, m)
+            if m + AHEAD < BANKS:
+                regroup_last(nc.vector.tensor_copy, m + AHEAD)
+            empty_and_store(nc.scalar.copy if m < BANKS - 1 else nc.vector.tensor_copy, m)

import concourse.mybir as mybir
from concourse.masks import make_identity

BF16 = mybir.dt.bfloat16
F32 = mybir.dt.float32
U32 = mybir.dt.uint32
U8 = mybir.dt.uint8
E4M3_X4 = mybir.dt.float8_e4m3fn_x4
E5M2_X4 = mybir.dt.float8_e5m2_x4

B, D, R = 2048, 1024, 512
P = 128
PACK = 4
K_PASS = P * PACK
PASSES = B // K_PASS
LAST = PASSES - 1
M_TILE = 128
BANKS = D // M_TILE
HALF = D // 2
AHEAD = 2
LAST_X_LOADS = ((0, HALF // 2), (HALF // 2, HALF // 2), (HALF, HALF))

DZ_RUN = 4
X_RUN = 8

FLOPS = 2 * B * D * R
BYTES = 2 * B * D + 2 * 4 * B * R + 2 * B + 2 + 4 * D * R


def rows_by_runs(rows, run):
    return rows.rearrange("p t (g i) -> p g t i", i=run)


def grouped_by_runs(grouped, run):
    return grouped.rearrange("p (g i) t -> p g t i", i=run)


def tile_polynomialtensorregression_pa_v_kernel(
    tc, X, U_0_0, U_1_0, U_1_1, U_2_0, U_2_1, U_2_2, C, beta, dot_2_1, dot_2_2, grad_out, out
):
    nc = tc.nc
    with tc.tile_pool(name="keep", bufs=1) as keep, tc.psum_pool(
        name="banks", bufs=1
    ) as banks, tc.manual_schedule():
        def load(source, c, first, width, dtype, name):
            piece = keep.tile([P, PACK, width], dtype, name="%s_%d_%d" % (name, c, first))
            nc.sync.dma_start(
                out=piece[:],
                in_=source[c * K_PASS : (c + 1) * K_PASS, first : first + width].rearrange(
                    "(p t) w -> p t w", t=PACK
                ),
            )
            return piece

        d1, d2, x_raw = [], [], []
        g_in = keep.tile([PASSES, K_PASS], BF16)
        c_in = keep.tile([PASSES, 3], BF16)
        for c in range(PASSES):
            if c < LAST:
                x_raw.append(load(X, c, 0, D, BF16, "x_raw"))
            if c == 0:
                nc.sync.dma_start(out=g_in[:], in_=grad_out.rearrange("(c k) -> c k", k=K_PASS))
                nc.sync.dma_start(out=c_in[:], in_=C.partition_broadcast(PASSES))
            d1.append(load(dot_2_1, c, 0, R, F32, "d1"))
            if c < LAST:
                d2.append(load(dot_2_2, c, 0, R, F32, "d2"))
        d2_last = [load(dot_2_2, LAST, first, R // 2, F32, "d2") for first in (0, R // 2)]
        x_last = [
            (first, width, load(X, LAST, first, width, BF16, "x_raw"))
            for first, width in LAST_X_LOADS
        ]

        acc = [banks.tile([P, R], F32, name="acc_%d" % m) for m in range(BANKS)]
        ident = keep.tile([P, P], BF16)
        make_identity(nc, ident[:])
        c_diag = keep.tile([P, PASSES], BF16)
        nc.vector.memset(c_diag[:], 0.0)
        g_stage = keep.tile([P, K_PASS], BF16)
        nc.vector.memset(g_stage[:], 0.0)
        borrowed = acc[BANKS - 1]
        row_factor = keep.tile([P, PACK, PASSES], F32)

        def stage_row_factors():
            nc.vector.tensor_copy(out=g_stage[0:PASSES, :], in_=g_in[:])
            nc.vector.tensor_scalar_mul(
                out=c_diag[0:PASSES, :], in0=ident[0:PASSES, 0:PASSES], scalar1=c_in[:, 2:3]
            )
            for t in range(PACK):
                nc.tensor.matmul(
                    out=borrowed[:, PASSES * t : PASSES * (t + 1)],
                    lhsT=g_stage[:, t::PACK],
                    rhs=c_diag[:],
                    start=True,
                    stop=True,
                )

        def fetch_row_factors():
            nc.vector.tensor_copy(
                out=row_factor[:].rearrange("p t c -> p (t c)"),
                in_=borrowed[:, 0 : PACK * PASSES],
            )

        dz_grouped = [
            keep.tile([P, R, PACK], BF16, name="dz_grouped_%d" % c, align_bytes=64)
            for c in range(PASSES)
        ]
        dz_codes = [
            keep.tile([P, R], U32, name="dz_codes_%d" % c, align_bytes=64) for c in range(PASSES)
        ]
        dz_scales = [
            keep.tile([P, R], U8, name="dz_scales_%d" % c, align_bytes=64) for c in range(PASSES)
        ]
        x_grouped = [
            keep.tile([P, D, PACK], BF16, name="x_grouped_%d" % c, align_bytes=64)
            for c in range(PASSES)
        ]
        x_codes = [
            keep.tile([P, D], U32, name="x_codes_%d" % c, align_bytes=64) for c in range(PASSES)
        ]
        x_scales = [
            keep.tile([P, D], U8, name="x_scales_%d" % c, align_bytes=64) for c in range(PASSES)
        ]

        def scale_row_on_scalar(c, t):
            nc.scalar.activation(
                out=d1[c][:, t, :],
                in_=d1[c][:, t, :],
                func=mybir.ActivationFunctionType.Copy,
                scale=row_factor[:, t, c : c + 1],
            )

        def scale_row_on_vector(c, t):
            nc.vector.tensor_scalar_mul(
                out=d1[c][:, t, :], in0=d1[c][:, t, :], scalar1=row_factor[:, t, c : c + 1]
            )

        def multiply_rows(c, factor, first=0, width=R):
            cols = slice(first, first + width)
            nc.vector.tensor_tensor(
                out=grouped_by_runs(dz_grouped[c][:, cols, :], DZ_RUN),
                in0=rows_by_runs(d1[c][:, :, cols], DZ_RUN),
                in1=rows_by_runs(factor[:], DZ_RUN),
                op=mybir.AluOpType.mult,
            )

        def quantize_dz(c, first=0, width=R):
            cols = slice(first, first + width)
            nc.vector.quantize_mx(
                out=dz_codes[c][:, cols].bitcast(E5M2_X4),
                scales=dz_scales[c][:, cols],
                in_=dz_grouped[c][:, cols, :].rearrange("p r t -> p (r t)"),
            )

        def regroup(engine_copy, c, rows, first, width):
            engine_copy(
                out=grouped_by_runs(x_grouped[c][:, first : first + width, :], X_RUN),
                in_=rows_by_runs(rows, X_RUN),
            )

        def regroup_last(engine_copy, m):
            first = m * M_TILE
            for left, loaded, piece in x_last:
                if left <= first < left + loaded:
                    rows = piece[:, :, first - left : first - left + M_TILE]
                    regroup(engine_copy, LAST, rows, first, M_TILE)

        def quantize_x(c, first, width):
            cols = slice(first, first + width)
            nc.vector.quantize_mx(
                out=x_codes[c][:, cols].bitcast(E4M3_X4),
                scales=x_scales[c][:, cols],
                in_=x_grouped[c][:, cols, :].rearrange("p w t -> p (w t)"),
            )

        def multiply(c, m):
            cols = slice(m * M_TILE, (m + 1) * M_TILE)
            nc.tensor.matmul_mx(
                out=acc[m][:],
                lhsT=x_codes[c][:, cols].bitcast(E4M3_X4),
                lhsT_scale=x_scales[c][:, cols],
                rhs=dz_codes[c][:].bitcast(E5M2_X4),
                rhs_scale=dz_scales[c][:],
                start=(c == 0),
                stop=(c == LAST),
            )

        def empty_and_store(engine_copy, m):
            result = keep.tile([P, R], F32, name="result_%d" % m)
            engine_copy(out=result[:], in_=acc[m][:])
            nc.sync.dma_start(out=out[m * M_TILE : (m + 1) * M_TILE, :], in_=result[:])

        def scale(c):
            for t in range(PACK // 2):
                scale_row_on_scalar(c, t)
            for t in range(PACK // 2, PACK):
                scale_row_on_vector(c, t)

        def finish(c):
            quantize_dz(c)
            for m in range(BANKS):
                multiply(c, m)

        for c in range(LAST):
            regroup(nc.vector.tensor_copy, c, x_raw[c][:, :, :HALF], 0, HALF)
            regroup(nc.scalar.copy, c, x_raw[c][:, :, HALF:], HALF, HALF)
            if c == 0:
                stage_row_factors()
            else:
                finish(c - 1)
            quantize_x(c, 0, HALF)
            if c == 0:
                fetch_row_factors()
            quantize_x(c, HALF, HALF)
            scale(c)
            multiply_rows(c, d2[c])

        scale(LAST)
        finish(LAST - 1)
        for m in range(AHEAD):
            regroup_last(nc.scalar.copy, m)
        for first, factor in zip((0, R // 2), d2_last):
            multiply_rows(LAST, factor, first, R // 2)
        for first in (0, R // 2):
            quantize_dz(LAST, first, R // 2)
        for m in range(BANKS):
            quantize_x(LAST, m * M_TILE, M_TILE)
            multiply(LAST, m)
            if m + AHEAD < BANKS:
                regroup_last(nc.vector.tensor_copy, m + AHEAD)
            empty_and_store(nc.scalar.copy if m < BANKS - 1 else nc.vector.tensor_copy, m)
